import numpy as np
import ml_dtypes


def mxq(x, axis, fmt="e4m3"):
    dtype, down = {"e4m3": (ml_dtypes.float8_e4m3fn, 7), "e5m2": (ml_dtypes.float8_e5m2, 14)}[fmt]
    v = np.moveaxis(np.asarray(x, np.float32).astype(ml_dtypes.bfloat16).astype(np.float64), axis, -1)
    blocks = v.reshape(v.shape[:-1] + (-1, 32))
    amax = np.abs(blocks).max(-1, keepdims=True)
    byte = np.maximum(np.where(amax > 0, np.frexp(amax)[1] - 1 + 127, 0) - down, 1)
    scale = np.exp2(byte - 127.0)
    codes = (blocks / scale).astype(np.float32).astype(dtype).astype(np.float64)
    return np.moveaxis((codes * scale).reshape(v.shape), -1, axis)


WIDE = False


def mx_kscale(k):
    if not WIDE:
        return np.ones(k)
    levels = np.array([10, -10, 5, -5, 0])
    a = np.random.permutation(np.resize(levels, k // 512 * 4)).reshape(k // 512, 4)
    idx = np.arange(k)
    return np.exp2(a[idx // 512, idx % 128 // 32])


BF16 = ml_dtypes.bfloat16


def bf(x):
    return np.asarray(x, np.float32).astype(BF16)


def f64(x):
    return np.asarray(x).astype(np.float64)


B, C, D, T, H, W, P = 1, 1024, 512, 8, 8, 8, 1
N = T * H * W
NP = T * (H // P) * (W // P)


def setup_inputs():
    s, t = mx_kscale(D), mx_kscale(NP)
    return {"theta_x": bf(np.random.standard_normal((B, D, N)) * 2.0 * s[None, :, None]),
            "phi_x": bf((1.03 + 0.7 * np.random.standard_normal((B, D, NP))) / s[None, :, None] * t[None, None, :]),
            "g_x": bf(0.15 * (1.03 + 0.7 * np.random.standard_normal((B, D, NP))) / t[None, None, :])}


def reference(theta_x, phi_x, g_x):
    f = (mxq(f64(theta_x), 1, "e4m3").transpose(0, 2, 1) @ mxq(f64(phi_x), 1, "e4m3")) / NP
    return mxq(f64(g_x), 2, "e4m3") @ mxq(f, 2, "e4m3").transpose(0, 2, 1)

@@ -1,0 +1,132 @@
+import concourse.mybir as mybir
+from concourse.masks import make_identity
+
+BF16 = mybir.dt.bfloat16
+F32 = mybir.dt.float32
+U32 = mybir.dt.uint32
+U8 = mybir.dt.uint8
+FP8X4 = mybir.dt.float8_e4m3fn_x4
+COPY = mybir.ActivationFunctionType.Copy
+
+P = 128
+PACK = 4
+SIZE = 512
+CHUNK = 128
+N_CHUNKS = SIZE // CHUNK
+HALF = SIZE // 2
+FLOPS = 2 * 2 * SIZE * SIZE * SIZE
+
+
+def quantise(nc, grouped, codes, scales):
+    nc.vector.quantize_mx(out=codes.bitcast(FP8X4), scales=scales, in_=grouped)
+
+
+def tile_nonlocalblocknd_pb_s_kernel(tc, theta_x, phi_x, g_x, out):
+    nc = tc.nc
+    theta = theta_x.flatten_outer_dims().rearrange("(p j) n -> p j n", j=PACK)
+    phi = phi_x.flatten_outer_dims().rearrange("(p j) m -> p j m", j=PACK)
+    g = g_x.flatten_outer_dims().rearrange("(p i) m -> p i m", i=PACK)
+    y = out.flatten_outer_dims().rearrange("(p i) n -> p i n", i=PACK)
+
+    with tc.tile_pool(name="keep", bufs=1) as keep, tc.tile_pool(
+        name="chunks", bufs=N_CHUNKS
+    ) as chunks, tc.psum_pool(name="banks", bufs=2) as banks:
+        phi_raw = keep.tile([P, PACK, SIZE], BF16)
+        nc.sync.dma_start(out=phi_raw[:], in_=phi)
+        g_rows = keep.tile([P, PACK, SIZE], BF16)
+        nc.sync.dma_start(out=g_rows[:], in_=g)
+        theta_raw = keep.tile([P, PACK, SIZE], BF16)
+        for h in range(2):
+            cols = slice(h * HALF, (h + 1) * HALF)
+            nc.sync.dma_start(out=theta_raw[:, :, cols], in_=theta[:, :, cols])
+
+        identity = keep.tile([P, P], F32)
+        make_identity(nc, identity[:])
+
+        table_in = keep.tile([P, 1], F32)
+        table_out = keep.tile([P, 1], F32)
+        nc.vector.memset(table_in[:], 0.0)
+        nc.scalar.activation(out=table_out[:], in_=table_in[:], func=COPY, scale=1.0)
+
+        phi_grouped = keep.tile([P, PACK, P, PACK], BF16, align_bytes=64)
+        nc.vector.tensor_copy(
+            out=phi_grouped[:].rearrange("p t c j -> p c j t"),
+            in_=phi_raw[:].rearrange("p j (c t) -> p c j t", t=PACK),
+        )
+        phi_codes = keep.tile([P, PACK, P], U32, align_bytes=64)
+        phi_scales = keep.tile([P, PACK, P], U8, align_bytes=64)
+        quantise(
+            nc,
+            phi_grouped[:].rearrange("p t c j -> p (t c j)"),
+            phi_codes[:].rearrange("p t c -> p (t c)"),
+            phi_scales[:].rearrange("p t c -> p (t c)"),
+        )
+
+        g_grouped = keep.tile([P, PACK * SIZE], BF16, align_bytes=64)
+        g_codes = keep.tile([P, PACK, P], U32, align_bytes=64)
+        g_scales = keep.tile([P, PACK, P], U8, align_bytes=64)
+        for b in range(2):
+            g_bank = banks.tile([P, 2, 2 * P], F32)
+            for i in range(2):
+                words = g_rows[:, 2 * b + i, :].bitcast(F32).rearrange("p (c u) -> p u c", u=2)
+                for u in range(2):
+                    nc.tensor.transpose(g_bank[:, u, i * P : (i + 1) * P], words[:, u, :], identity[:])
+            part = slice(b * 2 * SIZE, (b + 1) * 2 * SIZE)
+            nc.scalar.copy(
+                out=g_grouped[:, part].bitcast(F32).rearrange("c (x u) -> c x u", u=2),
+                in_=g_bank[:].rearrange("c u x -> c x u"),
+            )
+            quantise(
+                nc,
+                g_grouped[:, part],
+                g_codes[:, 2 * b : 2 * b + 2, :].rearrange("c i p -> c (i p)"),
+                g_scales[:, 2 * b : 2 * b + 2, :].rearrange("c i p -> c (i p)"),
+            )
+
+        for k in range(N_CHUNKS):
+            cols = slice(k * CHUNK, (k + 1) * CHUNK)
+            theta_grouped = chunks.tile([P, CHUNK, PACK], BF16, align_bytes=64)
+            nc.vector.tensor_copy(
+                out=theta_grouped[:].rearrange("p (c i) j -> p c j i", i=4),
+                in_=theta_raw[:, :, cols].rearrange("p j (c i) -> p c j i", i=4),
+            )
+            theta_codes = chunks.tile([P, CHUNK], U32, align_bytes=64)
+            theta_scales = chunks.tile([P, CHUNK], U8, align_bytes=64)
+            quantise(nc, theta_grouped[:].rearrange("p n j -> p (n j)"), theta_codes[:], theta_scales[:])
+
+            f_bank = banks.tile([P, PACK, CHUNK], F32)
+            for t in range(PACK):
+                nc.tensor.matmul_mx(
+                    out=f_bank[:, t, :],
+                    lhsT=phi_codes[:, t, :].bitcast(FP8X4),
+                    lhsT_scale=phi_scales[:, t, :],
+                    rhs=theta_codes[:].bitcast(FP8X4),
+                    rhs_scale=theta_scales[:],
+                    start=True,
+                    stop=True,
+                )
+            f_grouped = chunks.tile([P, CHUNK, PACK], BF16, align_bytes=64)
+            nc.scalar.activation(
+                out=f_grouped[:], in_=f_bank[:].rearrange("c t n -> c n t"), func=COPY, scale=1.0 / SIZE
+            )
+            f_codes = chunks.tile([P, CHUNK], U32, align_bytes=64)
+            f_scales = chunks.tile([P, CHUNK], U8, align_bytes=64)
+            quantise(nc, f_grouped[:].rearrange("c n t -> c (n t)"), f_codes[:], f_scales[:])
+
+            y_low = banks.tile([P, 2, CHUNK], F32)
+            y_high = banks.tile([P, 2, CHUNK], F32)
+            for i in range(PACK):
+                y_bank = y_low if i < 2 else y_high
+                nc.tensor.matmul_mx(
+                    out=y_bank[:, i % 2, :],
+                    lhsT=g_codes[:, i, :].bitcast(FP8X4),
+                    lhsT_scale=g_scales[:, i, :],
+                    rhs=f_codes[:].bitcast(FP8X4),
+                    rhs_scale=f_scales[:],
+                    start=True,
+                    stop=True,
+                )
+            y_sb = chunks.tile([P, PACK, CHUNK], F32)
+            nc.vector.tensor_copy(out=y_sb[:, 0:2, :], in_=y_low[:])
+            nc.scalar.copy(out=y_sb[:, 2:4, :], in_=y_high[:])
+            nc.sync.dma_start(out=y[:, :, cols], in_=y_sb[:])

@@ -14,6 +14,7 @@ SIZE = 512
 CHUNK = 128
 N_CHUNKS = SIZE // CHUNK
 HALF = SIZE // 2
+PHI_SPLIT = 88
 FLOPS = 2 * 2 * SIZE * SIZE * SIZE
 
 
@@ -28,9 +29,9 @@ def tile_nonlocalblocknd_pb_s_kernel(tc, theta_x, phi_x, g_x, out):
     g = g_x.flatten_outer_dims().rearrange("(p i) m -> p i m", i=PACK)
     y = out.flatten_outer_dims().rearrange("(p i) n -> p i n", i=PACK)
 
-    with tc.tile_pool(name="keep", bufs=1) as keep, tc.tile_pool(
-        name="chunks", bufs=N_CHUNKS
-    ) as chunks, tc.psum_pool(name="banks", bufs=2) as banks:
+    with tc.tile_pool(name="keep", bufs=1) as keep, tc.psum_pool(
+        name="banks", bufs=2
+    ) as banks, tc.manual_schedule():
         phi_raw = keep.tile([P, PACK, SIZE], BF16)
         nc.sync.dma_start(out=phi_raw[:], in_=phi)
         g_rows = keep.tile([P, PACK, SIZE], BF16)
@@ -49,10 +50,10 @@ def tile_nonlocalblocknd_pb_s_kernel(tc, theta_x, phi_x, g_x, out):
         nc.scalar.activation(out=table_out[:], in_=table_in[:], func=COPY, scale=1.0)
 
         phi_grouped = keep.tile([P, PACK, P, PACK], BF16, align_bytes=64)
-        nc.vector.tensor_copy(
-            out=phi_grouped[:].rearrange("p t c j -> p c j t"),
-            in_=phi_raw[:].rearrange("p j (c t) -> p c j t", t=PACK),
-        )
+        phi_sorted = phi_raw[:].rearrange("p j (c t) -> p c j t", t=PACK)
+        phi_target = phi_grouped[:].rearrange("p t c j -> p c j t")
+        nc.vector.tensor_copy(out=phi_target[:, 0:PHI_SPLIT], in_=phi_sorted[:, 0:PHI_SPLIT])
+        nc.scalar.copy(out=phi_target[:, PHI_SPLIT:P], in_=phi_sorted[:, PHI_SPLIT:P])
         phi_codes = keep.tile([P, PACK, P], U32, align_bytes=64)
         phi_scales = keep.tile([P, PACK, P], U8, align_bytes=64)
         quantise(
@@ -62,71 +63,104 @@ def tile_nonlocalblocknd_pb_s_kernel(tc, theta_x, phi_x, g_x, out):
             phi_scales[:].rearrange("p t c -> p (t c)"),
         )
 
+        theta_grouped = keep.tile([P, SIZE, PACK], BF16, align_bytes=64)
+        theta_codes = keep.tile([P, SIZE], U32, align_bytes=64)
+        theta_scales = keep.tile([P, SIZE], U8, align_bytes=64)
+
+        def prepare_theta(k):
+            cols = slice(k * CHUNK, (k + 1) * CHUNK)
+            nc.vector.tensor_copy(
+                out=theta_grouped[:, cols, :].rearrange("p (c i) j -> p c j i", i=4),
+                in_=theta_raw[:, :, cols].rearrange("p j (c i) -> p c j i", i=4),
+            )
+            quantise(
+                nc,
+                theta_grouped[:, cols, :].rearrange("p n j -> p (n j)"),
+                theta_codes[:, cols],
+                theta_scales[:, cols],
+            )
+
         g_grouped = keep.tile([P, PACK * SIZE], BF16, align_bytes=64)
         g_codes = keep.tile([P, PACK, P], U32, align_bytes=64)
         g_scales = keep.tile([P, PACK, P], U8, align_bytes=64)
-        for b in range(2):
+
+        def transpose_g(b):
             g_bank = banks.tile([P, 2, 2 * P], F32)
             for i in range(2):
                 words = g_rows[:, 2 * b + i, :].bitcast(F32).rearrange("p (c u) -> p u c", u=2)
                 for u in range(2):
                     nc.tensor.transpose(g_bank[:, u, i * P : (i + 1) * P], words[:, u, :], identity[:])
-            part = slice(b * 2 * SIZE, (b + 1) * 2 * SIZE)
             nc.scalar.copy(
-                out=g_grouped[:, part].bitcast(F32).rearrange("c (x u) -> c x u", u=2),
+                out=g_grouped[:, b * 2 * SIZE : (b + 1) * 2 * SIZE]
+                .bitcast(F32)
+                .rearrange("c (x u) -> c x u", u=2),
                 in_=g_bank[:].rearrange("c u x -> c x u"),
             )
+
+        def quantise_g(b):
             quantise(
                 nc,
-                g_grouped[:, part],
+                g_grouped[:, b * 2 * SIZE : (b + 1) * 2 * SIZE],
                 g_codes[:, 2 * b : 2 * b + 2, :].rearrange("c i p -> c (i p)"),
                 g_scales[:, 2 * b : 2 * b + 2, :].rearrange("c i p -> c (i p)"),
             )
 
-        for k in range(N_CHUNKS):
-            cols = slice(k * CHUNK, (k + 1) * CHUNK)
-            theta_grouped = chunks.tile([P, CHUNK, PACK], BF16, align_bytes=64)
-            nc.vector.tensor_copy(
-                out=theta_grouped[:].rearrange("p (c i) j -> p c j i", i=4),
-                in_=theta_raw[:, :, cols].rearrange("p j (c i) -> p c j i", i=4),
-            )
-            theta_codes = chunks.tile([P, CHUNK], U32, align_bytes=64)
-            theta_scales = chunks.tile([P, CHUNK], U8, align_bytes=64)
-            quantise(nc, theta_grouped[:].rearrange("p n j -> p (n j)"), theta_codes[:], theta_scales[:])
+        f_grouped = keep.tile([P, SIZE, PACK], BF16, align_bytes=64)
+        f_codes = keep.tile([P, SIZE], U32, align_bytes=64)
+        f_scales = keep.tile([P, SIZE], U8, align_bytes=64)
+        y_sb = keep.tile([P, PACK, SIZE], F32)
 
+        def first_product(k):
+            cols = slice(k * CHUNK, (k + 1) * CHUNK)
             f_bank = banks.tile([P, PACK, CHUNK], F32)
             for t in range(PACK):
                 nc.tensor.matmul_mx(
                     out=f_bank[:, t, :],
                     lhsT=phi_codes[:, t, :].bitcast(FP8X4),
                     lhsT_scale=phi_scales[:, t, :],
-                    rhs=theta_codes[:].bitcast(FP8X4),
-                    rhs_scale=theta_scales[:],
+                    rhs=theta_codes[:, cols].bitcast(FP8X4),
+                    rhs_scale=theta_scales[:, cols],
                     start=True,
                     stop=True,
                 )
-            f_grouped = chunks.tile([P, CHUNK, PACK], BF16, align_bytes=64)
             nc.scalar.activation(
-                out=f_grouped[:], in_=f_bank[:].rearrange("c t n -> c n t"), func=COPY, scale=1.0 / SIZE
+                out=f_grouped[:, cols, :],
+                in_=f_bank[:].rearrange("c t n -> c n t"),
+                func=COPY,
+                scale=1.0 / SIZE,
             )
-            f_codes = chunks.tile([P, CHUNK], U32, align_bytes=64)
-            f_scales = chunks.tile([P, CHUNK], U8, align_bytes=64)
-            quantise(nc, f_grouped[:].rearrange("c n t -> c (n t)"), f_codes[:], f_scales[:])
 
-            y_low = banks.tile([P, 2, CHUNK], F32)
-            y_high = banks.tile([P, 2, CHUNK], F32)
-            for i in range(PACK):
-                y_bank = y_low if i < 2 else y_high
+        def quantise_f(k):
+            cols = slice(k * CHUNK, (k + 1) * CHUNK)
+            quantise(
+                nc, f_grouped[:, cols, :].rearrange("c n t -> c (n t)"), f_codes[:, cols], f_scales[:, cols]
+            )
+
+        def second_product(i):
+            y_left = banks.tile([P, HALF], F32)
+            y_right = banks.tile([P, HALF], F32)
+            for y_bank, cols in ((y_left, slice(0, HALF)), (y_right, slice(HALF, SIZE))):
                 nc.tensor.matmul_mx(
-                    out=y_bank[:, i % 2, :],
+                    out=y_bank[:],
                     lhsT=g_codes[:, i, :].bitcast(FP8X4),
                     lhsT_scale=g_scales[:, i, :],
-                    rhs=f_codes[:].bitcast(FP8X4),
-                    rhs_scale=f_scales[:],
+                    rhs=f_codes[:, cols].bitcast(FP8X4),
+                    rhs_scale=f_scales[:, cols],
                     start=True,
                     stop=True,
                 )
-            y_sb = chunks.tile([P, PACK, CHUNK], F32)
-            nc.vector.tensor_copy(out=y_sb[:, 0:2, :], in_=y_low[:])
-            nc.scalar.copy(out=y_sb[:, 2:4, :], in_=y_high[:])
-            nc.sync.dma_start(out=y[:, :, cols], in_=y_sb[:])
+            nc.vector.tensor_copy(out=y_sb[:, i, 0:HALF], in_=y_left[:])
+            nc.scalar.copy(out=y_sb[:, i, HALF:SIZE], in_=y_right[:])
+            nc.sync.dma_start(out=y[:, i, :], in_=y_sb[:, i, :])
+
+        transpose_g(0)
+        transpose_g(1)
+        for k in range(N_CHUNKS):
+            prepare_theta(k)
+            first_product(k)
+        quantise_g(0)
+        quantise_g(1)
+        for k in range(N_CHUNKS):
+            quantise_f(k)
+        for i in range(PACK):
+            second_product(i)

@@ -30,7 +30,7 @@ def tile_nonlocalblocknd_pb_s_kernel(tc, theta_x, phi_x, g_x, out):
     y = out.flatten_outer_dims().rearrange("(p i) n -> p i n", i=PACK)
 
     with tc.tile_pool(name="keep", bufs=1) as keep, tc.psum_pool(
-        name="banks", bufs=2
+        name="banks", bufs=8
     ) as banks, tc.manual_schedule():
         phi_raw = keep.tile([P, PACK, SIZE], BF16)
         nc.sync.dma_start(out=phi_raw[:], in_=phi)
@@ -85,7 +85,7 @@ def tile_nonlocalblocknd_pb_s_kernel(tc, theta_x, phi_x, g_x, out):
         g_scales = keep.tile([P, PACK, P], U8, align_bytes=64)
 
         def transpose_g(b):
-            g_bank = banks.tile([P, 2, 2 * P], F32)
+            g_bank = banks.tile([P, 2, 2 * P], F32, tag="bank")
             for i in range(2):
                 words = g_rows[:, 2 * b + i, :].bitcast(F32).rearrange("p (c u) -> p u c", u=2)
                 for u in range(2):
@@ -112,7 +112,7 @@ def tile_nonlocalblocknd_pb_s_kernel(tc, theta_x, phi_x, g_x, out):
 
         def first_product(k):
             cols = slice(k * CHUNK, (k + 1) * CHUNK)
-            f_bank = banks.tile([P, PACK, CHUNK], F32)
+            f_bank = banks.tile([P, PACK, CHUNK], F32, tag="bank")
             for t in range(PACK):
                 nc.tensor.matmul_mx(
                     out=f_bank[:, t, :],
@@ -136,22 +136,23 @@ def tile_nonlocalblocknd_pb_s_kernel(tc, theta_x, phi_x, g_x, out):
                 nc, f_grouped[:, cols, :].rearrange("c n t -> c (n t)"), f_codes[:, cols], f_scales[:, cols]
             )
 
-        def second_product(i):
-            y_left = banks.tile([P, HALF], F32)
-            y_right = banks.tile([P, HALF], F32)
-            for y_bank, cols in ((y_left, slice(0, HALF)), (y_right, slice(HALF, SIZE))):
-                nc.tensor.matmul_mx(
-                    out=y_bank[:],
-                    lhsT=g_codes[:, i, :].bitcast(FP8X4),
-                    lhsT_scale=g_scales[:, i, :],
-                    rhs=f_codes[:, cols].bitcast(FP8X4),
-                    rhs_scale=f_scales[:, cols],
-                    start=True,
-                    stop=True,
-                )
-            nc.vector.tensor_copy(out=y_sb[:, i, 0:HALF], in_=y_left[:])
-            nc.scalar.copy(out=y_sb[:, i, HALF:SIZE], in_=y_right[:])
-            nc.sync.dma_start(out=y[:, i, :], in_=y_sb[:, i, :])
+        def second_product(h):
+            cols = slice(h * HALF, (h + 1) * HALF)
+            for b, copy_out in ((0, nc.vector.tensor_copy), (1, nc.scalar.copy)):
+                y_bank = banks.tile([P, 2, HALF], F32, tag="bank")
+                for i in range(2):
+                    nc.tensor.matmul_mx(
+                        out=y_bank[:, i, :],
+                        lhsT=g_codes[:, 2 * b + i, :].bitcast(FP8X4),
+                        lhsT_scale=g_scales[:, 2 * b + i, :],
+                        rhs=f_codes[:, cols].bitcast(FP8X4),
+                        rhs_scale=f_scales[:, cols],
+                        start=True,
+                        stop=True,
+                    )
+                rows = slice(2 * b, 2 * b + 2)
+                copy_out(out=y_sb[:, rows, cols], in_=y_bank[:])
+                nc.sync.dma_start(out=y[:, rows, cols], in_=y_sb[:, rows, cols])
 
         transpose_g(0)
         transpose_g(1)
@@ -160,7 +161,9 @@ def tile_nonlocalblocknd_pb_s_kernel(tc, theta_x, phi_x, g_x, out):
             first_product(k)
         quantise_g(0)
         quantise_g(1)
-        for k in range(N_CHUNKS):
-            quantise_f(k)
-        for i in range(PACK):
-            second_product(i)
+        quantise_f(0)
+        quantise_f(1)
+        quantise_f(2)
+        second_product(0)
+        quantise_f(3)
+        second_product(1)

@@ -15,6 +15,7 @@ CHUNK = 128
 N_CHUNKS = SIZE // CHUNK
 HALF = SIZE // 2
 PHI_SPLIT = 88
+WARM_UP_PASSES = 12
 FLOPS = 2 * 2 * SIZE * SIZE * SIZE
 
 
@@ -35,11 +36,10 @@ def tile_nonlocalblocknd_pb_s_kernel(tc, theta_x, phi_x, g_x, out):
         phi_raw = keep.tile([P, PACK, SIZE], BF16)
         nc.sync.dma_start(out=phi_raw[:], in_=phi)
         g_rows = keep.tile([P, PACK, SIZE], BF16)
-        nc.sync.dma_start(out=g_rows[:], in_=g)
         theta_raw = keep.tile([P, PACK, SIZE], BF16)
-        for h in range(2):
-            cols = slice(h * HALF, (h + 1) * HALF)
-            nc.sync.dma_start(out=theta_raw[:, :, cols], in_=theta[:, :, cols])
+        nc.sync.dma_start(out=theta_raw[:, :, 0:HALF], in_=theta[:, :, 0:HALF])
+        nc.sync.dma_start(out=g_rows[:], in_=g)
+        nc.sync.dma_start(out=theta_raw[:, :, HALF:SIZE], in_=theta[:, :, HALF:SIZE])
 
         identity = keep.tile([P, P], F32)
         make_identity(nc, identity[:])
@@ -49,6 +49,23 @@ def tile_nonlocalblocknd_pb_s_kernel(tc, theta_x, phi_x, g_x, out):
         nc.vector.memset(table_in[:], 0.0)
         nc.scalar.activation(out=table_out[:], in_=table_in[:], func=COPY, scale=1.0)
 
+        idle_grouped = keep.tile([P, HALF * PACK], BF16, align_bytes=64)
+        idle_codes = keep.tile([P, HALF], U32, align_bytes=64)
+        idle_scales = keep.tile([P, HALF], U8, align_bytes=64)
+        nc.vector.memset(idle_grouped[:], 0.0)
+        quantise(nc, idle_grouped[:], idle_codes[:], idle_scales[:])
+        idle_bank = banks.tile([P, HALF], F32, tag="bank")
+        for w in range(WARM_UP_PASSES):
+            nc.tensor.matmul_mx(
+                out=idle_bank[:],
+                lhsT=idle_codes[:, 0:P].bitcast(FP8X4),
+                lhsT_scale=idle_scales[:, 0:P],
+                rhs=idle_codes[:].bitcast(FP8X4),
+                rhs_scale=idle_scales[:],
+                start=True,
+                stop=True,
+            )
+
         phi_grouped = keep.tile([P, PACK, P, PACK], BF16, align_bytes=64)
         phi_sorted = phi_raw[:].rearrange("p j (c t) -> p c j t", t=PACK)
         phi_target = phi_grouped[:].rearrange("p t c j -> p c j t")
@@ -56,23 +73,27 @@ def tile_nonlocalblocknd_pb_s_kernel(tc, theta_x, phi_x, g_x, out):
         nc.scalar.copy(out=phi_target[:, PHI_SPLIT:P], in_=phi_sorted[:, PHI_SPLIT:P])
         phi_codes = keep.tile([P, PACK, P], U32, align_bytes=64)
         phi_scales = keep.tile([P, PACK, P], U8, align_bytes=64)
-        quantise(
-            nc,
-            phi_grouped[:].rearrange("p t c j -> p (t c j)"),
-            phi_codes[:].rearrange("p t c -> p (t c)"),
-            phi_scales[:].rearrange("p t c -> p (t c)"),
-        )
+
+        def quantise_phi():
+            quantise(
+                nc,
+                phi_grouped[:].rearrange("p t c j -> p (t c j)"),
+                phi_codes[:].rearrange("p t c -> p (t c)"),
+                phi_scales[:].rearrange("p t c -> p (t c)"),
+            )
 
         theta_grouped = keep.tile([P, SIZE, PACK], BF16, align_bytes=64)
         theta_codes = keep.tile([P, SIZE], U32, align_bytes=64)
         theta_scales = keep.tile([P, SIZE], U8, align_bytes=64)
 
-        def prepare_theta(k):
-            cols = slice(k * CHUNK, (k + 1) * CHUNK)
-            nc.vector.tensor_copy(
+        def regroup_theta(copy, cols):
+            copy(
                 out=theta_grouped[:, cols, :].rearrange("p (c i) j -> p c j i", i=4),
                 in_=theta_raw[:, :, cols].rearrange("p j (c i) -> p c j i", i=4),
             )
+
+        def quantise_theta(h):
+            cols = slice(h * HALF, (h + 1) * HALF)
             quantise(
                 nc,
                 theta_grouped[:, cols, :].rearrange("p n j -> p (n j)"),
@@ -84,17 +105,22 @@ def tile_nonlocalblocknd_pb_s_kernel(tc, theta_x, phi_x, g_x, out):
         g_codes = keep.tile([P, PACK, P], U32, align_bytes=64)
         g_scales = keep.tile([P, PACK, P], U8, align_bytes=64)
 
+        g_banks = {}
+
         def transpose_g(b):
             g_bank = banks.tile([P, 2, 2 * P], F32, tag="bank")
+            g_banks[b] = g_bank
             for i in range(2):
                 words = g_rows[:, 2 * b + i, :].bitcast(F32).rearrange("p (c u) -> p u c", u=2)
                 for u in range(2):
                     nc.tensor.transpose(g_bank[:, u, i * P : (i + 1) * P], words[:, u, :], identity[:])
+
+        def regroup_g(b):
             nc.scalar.copy(
                 out=g_grouped[:, b * 2 * SIZE : (b + 1) * 2 * SIZE]
                 .bitcast(F32)
                 .rearrange("c (x u) -> c x u", u=2),
-                in_=g_bank[:].rearrange("c u x -> c x u"),
+                in_=g_banks[b][:].rearrange("c u x -> c x u"),
             )
 
         def quantise_g(b):
@@ -110,9 +136,12 @@ def tile_nonlocalblocknd_pb_s_kernel(tc, theta_x, phi_x, g_x, out):
         f_scales = keep.tile([P, SIZE], U8, align_bytes=64)
         y_sb = keep.tile([P, PACK, SIZE], F32)
 
+        f_banks = {}
+
         def first_product(k):
             cols = slice(k * CHUNK, (k + 1) * CHUNK)
             f_bank = banks.tile([P, PACK, CHUNK], F32, tag="bank")
+            f_banks[k] = f_bank
             for t in range(PACK):
                 nc.tensor.matmul_mx(
                     out=f_bank[:, t, :],
@@ -123,47 +152,73 @@ def tile_nonlocalblocknd_pb_s_kernel(tc, theta_x, phi_x, g_x, out):
                     start=True,
                     stop=True,
                 )
-            nc.scalar.activation(
-                out=f_grouped[:, cols, :],
-                in_=f_bank[:].rearrange("c t n -> c n t"),
-                func=COPY,
-                scale=1.0 / SIZE,
-            )
 
-        def quantise_f(k):
+        def scale_f(k, on_vector):
             cols = slice(k * CHUNK, (k + 1) * CHUNK)
+            source = f_banks[k][:].rearrange("c t n -> c n t")
+            if on_vector:
+                nc.vector.tensor_scalar_mul(out=f_grouped[:, cols, :], in0=source, scalar1=1.0 / SIZE)
+            else:
+                nc.scalar.activation(out=f_grouped[:, cols, :], in_=source, func=COPY, scale=1.0 / SIZE)
+
+        def quantise_f(cols):
             quantise(
                 nc, f_grouped[:, cols, :].rearrange("c n t -> c (n t)"), f_codes[:, cols], f_scales[:, cols]
             )
 
-        def second_product(h):
-            cols = slice(h * HALF, (h + 1) * HALF)
-            for b, copy_out in ((0, nc.vector.tensor_copy), (1, nc.scalar.copy)):
-                y_bank = banks.tile([P, 2, HALF], F32, tag="bank")
-                for i in range(2):
-                    nc.tensor.matmul_mx(
-                        out=y_bank[:, i, :],
-                        lhsT=g_codes[:, 2 * b + i, :].bitcast(FP8X4),
-                        lhsT_scale=g_scales[:, 2 * b + i, :],
-                        rhs=f_codes[:, cols].bitcast(FP8X4),
-                        rhs_scale=f_scales[:, cols],
-                        start=True,
-                        stop=True,
-                    )
-                rows = slice(2 * b, 2 * b + 2)
-                copy_out(out=y_sb[:, rows, cols], in_=y_bank[:])
-                nc.sync.dma_start(out=y[:, rows, cols], in_=y_sb[:, rows, cols])
+        y_banks = {}
 
+        def second_product(cols, b):
+            width = cols.stop - cols.start
+            y_bank = banks.tile([P, 2, width], F32, tag="bank")
+            y_banks[cols.start, b] = y_bank
+            for i in range(2):
+                nc.tensor.matmul_mx(
+                    out=y_bank[:, i, :],
+                    lhsT=g_codes[:, 2 * b + i, :].bitcast(FP8X4),
+                    lhsT_scale=g_scales[:, 2 * b + i, :],
+                    rhs=f_codes[:, cols].bitcast(FP8X4),
+                    rhs_scale=f_scales[:, cols],
+                    start=True,
+                    stop=True,
+                )
+
+        def store_y(cols, b, copy):
+            rows = slice(2 * b, 2 * b + 2)
+            copy(out=y_sb[:, rows, cols], in_=y_banks[cols.start, b][:])
+            nc.sync.dma_start(out=y[:, rows, cols], in_=y_sb[:, rows, cols])
+
+        first_half, third, fourth = slice(0, HALF), slice(HALF, HALF + CHUNK), slice(HALF + CHUNK, SIZE)
+        regroup_theta(nc.scalar.copy, slice(0, CHUNK))
+        regroup_theta(nc.vector.tensor_copy, slice(CHUNK, HALF))
+        quantise_phi()
+        quantise_theta(0)
         transpose_g(0)
+        first_product(0)
+        first_product(1)
         transpose_g(1)
-        for k in range(N_CHUNKS):
-            prepare_theta(k)
-            first_product(k)
+        regroup_theta(nc.vector.tensor_copy, slice(HALF, SIZE))
+        regroup_g(0)
+        scale_f(0, True)
+        scale_f(1, False)
         quantise_g(0)
+        quantise_theta(1)
+        first_product(2)
+        first_product(3)
+        regroup_g(1)
+        quantise_f(first_half)
         quantise_g(1)
-        quantise_f(0)
-        quantise_f(1)
-        quantise_f(2)
-        second_product(0)
-        quantise_f(3)
-        second_product(1)
+        scale_f(2, False)
+        second_product(first_half, 0)
+        second_product(first_half, 1)
+        scale_f(3, True)
+        store_y(first_half, 0, nc.scalar.copy)
+        quantise_f(third)
+        quantise_f(fourth)
+        for cols in (third, fourth):
+            for b in range(2):
+                second_product(cols, b)
+        store_y(first_half, 1, nc.vector.tensor_copy)
+        for cols in (third, fourth):
+            store_y(cols, 0, nc.scalar.copy)
+            store_y(cols, 1, nc.vector.tensor_copy)

@@ -15,7 +15,7 @@ CHUNK = 128
 N_CHUNKS = SIZE // CHUNK
 HALF = SIZE // 2
 PHI_SPLIT = 88
-WARM_UP_PASSES = 12
+WARM_UP_PASSES = 24
 FLOPS = 2 * 2 * SIZE * SIZE * SIZE
 
 
@@ -37,9 +37,11 @@ def tile_nonlocalblocknd_pb_s_kernel(tc, theta_x, phi_x, g_x, out):
         nc.sync.dma_start(out=phi_raw[:], in_=phi)
         g_rows = keep.tile([P, PACK, SIZE], BF16)
         theta_raw = keep.tile([P, PACK, SIZE], BF16)
-        nc.sync.dma_start(out=theta_raw[:, :, 0:HALF], in_=theta[:, :, 0:HALF])
-        nc.sync.dma_start(out=g_rows[:], in_=g)
-        nc.sync.dma_start(out=theta_raw[:, :, HALF:SIZE], in_=theta[:, :, HALF:SIZE])
+        for h in range(2):
+            cols = slice(h * HALF, (h + 1) * HALF)
+            rows = slice(2 * h, 2 * h + 2)
+            nc.sync.dma_start(out=theta_raw[:, :, cols], in_=theta[:, :, cols])
+            nc.sync.dma_start(out=g_rows[:, rows, :], in_=g[:, rows, :])
 
         identity = keep.tile([P, P], F32)
         make_identity(nc, identity[:])
@@ -49,17 +51,17 @@ def tile_nonlocalblocknd_pb_s_kernel(tc, theta_x, phi_x, g_x, out):
         nc.vector.memset(table_in[:], 0.0)
         nc.scalar.activation(out=table_out[:], in_=table_in[:], func=COPY, scale=1.0)
 
-        idle_grouped = keep.tile([P, HALF * PACK], BF16, align_bytes=64)
-        idle_codes = keep.tile([P, HALF], U32, align_bytes=64)
-        idle_scales = keep.tile([P, HALF], U8, align_bytes=64)
-        nc.vector.memset(idle_grouped[:], 0.0)
+        idle_grouped = keep.tile([P, PACK * P], BF16, align_bytes=64)
+        idle_codes = keep.tile([P, P], U32, align_bytes=64)
+        idle_scales = keep.tile([P, P], U8, align_bytes=64)
+        nc.vector.memset(idle_grouped[:].bitcast(U32), 0)
         quantise(nc, idle_grouped[:], idle_codes[:], idle_scales[:])
-        idle_bank = banks.tile([P, HALF], F32, tag="bank")
+        idle_bank = banks.tile([P, P], F32, tag="bank")
         for w in range(WARM_UP_PASSES):
             nc.tensor.matmul_mx(
                 out=idle_bank[:],
-                lhsT=idle_codes[:, 0:P].bitcast(FP8X4),
-                lhsT_scale=idle_scales[:, 0:P],
+                lhsT=idle_codes[:].bitcast(FP8X4),
+                lhsT_scale=idle_scales[:],
                 rhs=idle_codes[:].bitcast(FP8X4),
                 rhs_scale=idle_scales[:],
                 start=True,
@@ -188,37 +190,38 @@ def tile_nonlocalblocknd_pb_s_kernel(tc, theta_x, phi_x, g_x, out):
             copy(out=y_sb[:, rows, cols], in_=y_banks[cols.start, b][:])
             nc.sync.dma_start(out=y[:, rows, cols], in_=y_sb[:, rows, cols])
 
-        first_half, third, fourth = slice(0, HALF), slice(HALF, HALF + CHUNK), slice(HALF + CHUNK, SIZE)
-        regroup_theta(nc.scalar.copy, slice(0, CHUNK))
-        regroup_theta(nc.vector.tensor_copy, slice(CHUNK, HALF))
+        halves = (slice(0, HALF), slice(HALF, SIZE))
+        chunks = [slice(k * CHUNK, (k + 1) * CHUNK) for k in range(N_CHUNKS)]
+        regroup_theta(nc.vector.tensor_copy, chunks[0])
+        regroup_theta(nc.scalar.copy, chunks[1])
         quantise_phi()
         quantise_theta(0)
         transpose_g(0)
         first_product(0)
         first_product(1)
         transpose_g(1)
-        regroup_theta(nc.vector.tensor_copy, slice(HALF, SIZE))
+        regroup_theta(nc.vector.tensor_copy, chunks[2])
+        regroup_theta(nc.scalar.copy, chunks[3])
         regroup_g(0)
         scale_f(0, True)
         scale_f(1, False)
-        quantise_g(0)
         quantise_theta(1)
+        quantise_g(0)
         first_product(2)
         first_product(3)
         regroup_g(1)
-        quantise_f(first_half)
-        quantise_g(1)
+        quantise_f(chunks[0])
+        quantise_f(chunks[1])
         scale_f(2, False)
-        second_product(first_half, 0)
-        second_product(first_half, 1)
-        scale_f(3, True)
-        store_y(first_half, 0, nc.scalar.copy)
-        quantise_f(third)
-        quantise_f(fourth)
-        for cols in (third, fourth):
-            for b in range(2):
-                second_product(cols, b)
-        store_y(first_half, 1, nc.vector.tensor_copy)
-        for cols in (third, fourth):
-            store_y(cols, 0, nc.scalar.copy)
-            store_y(cols, 1, nc.vector.tensor_copy)
+        scale_f(3, False)
+        second_product(halves[0], 0)
+        quantise_g(1)
+        second_product(halves[0], 1)
+        store_y(halves[0], 0, nc.vector.tensor_copy)
+        store_y(halves[0], 1, nc.scalar.copy)
+        quantise_f(chunks[2])
+        quantise_f(chunks[3])
+        second_product(halves[1], 0)
+        second_product(halves[1], 1)
+        store_y(halves[1], 0, nc.vector.tensor_copy)
+        store_y(halves[1], 1, nc.scalar.copy)

@@ -34,7 +34,9 @@ def tile_nonlocalblocknd_pb_s_kernel(tc, theta_x, phi_x, g_x, out):
         name="banks", bufs=8
     ) as banks, tc.manual_schedule():
         phi_raw = keep.tile([P, PACK, SIZE], BF16)
-        nc.sync.dma_start(out=phi_raw[:], in_=phi)
+        for h in range(2):
+            rows = slice(2 * h, 2 * h + 2)
+            nc.sync.dma_start(out=phi_raw[:, rows, :], in_=phi[:, rows, :])
         g_rows = keep.tile([P, PACK, SIZE], BF16)
         theta_raw = keep.tile([P, PACK, SIZE], BF16)
         for h in range(2):
@@ -71,8 +73,10 @@ def tile_nonlocalblocknd_pb_s_kernel(tc, theta_x, phi_x, g_x, out):
         phi_grouped = keep.tile([P, PACK, P, PACK], BF16, align_bytes=64)
         phi_sorted = phi_raw[:].rearrange("p j (c t) -> p c j t", t=PACK)
         phi_target = phi_grouped[:].rearrange("p t c j -> p c j t")
-        nc.vector.tensor_copy(out=phi_target[:, 0:PHI_SPLIT], in_=phi_sorted[:, 0:PHI_SPLIT])
-        nc.scalar.copy(out=phi_target[:, PHI_SPLIT:P], in_=phi_sorted[:, PHI_SPLIT:P])
+        for h in range(2):
+            rows = slice(2 * h, 2 * h + 2)
+            for copy, columns in ((nc.vector.tensor_copy, slice(0, PHI_SPLIT)), (nc.scalar.copy, slice(PHI_SPLIT, P))):
+                copy(out=phi_target[:, columns, rows, :], in_=phi_sorted[:, columns, rows, :])
         phi_codes = keep.tile([P, PACK, P], U32, align_bytes=64)
         phi_scales = keep.tile([P, PACK, P], U8, align_bytes=64)
 
@@ -171,12 +175,14 @@ def tile_nonlocalblocknd_pb_s_kernel(tc, theta_x, phi_x, g_x, out):
         y_banks = {}
 
         def second_product(cols, b):
-            width = cols.stop - cols.start
-            y_bank = banks.tile([P, 2, width], F32, tag="bank")
-            y_banks[cols.start, b] = y_bank
+            half = cols.start // HALF
+            if (half, b) not in y_banks:
+                y_bank = banks.tile([P, 2, HALF], F32, tag="bank")
+                y_banks[half, b] = y_bank
+            first = cols.start - half * HALF
             for i in range(2):
                 nc.tensor.matmul_mx(
-                    out=y_bank[:, i, :],
+                    out=y_banks[half, b][:, i, first : first + cols.stop - cols.start],
                     lhsT=g_codes[:, 2 * b + i, :].bitcast(FP8X4),
                     lhsT_scale=g_scales[:, 2 * b + i, :],
                     rhs=f_codes[:, cols].bitcast(FP8X4),
@@ -185,9 +191,10 @@ def tile_nonlocalblocknd_pb_s_kernel(tc, theta_x, phi_x, g_x, out):
                     stop=True,
                 )
 
-        def store_y(cols, b, copy):
+        def store_y(half, b, copy):
+            cols = halves[half]
             rows = slice(2 * b, 2 * b + 2)
-            copy(out=y_sb[:, rows, cols], in_=y_banks[cols.start, b][:])
+            copy(out=y_sb[:, rows, cols], in_=y_banks[half, b][:])
             nc.sync.dma_start(out=y[:, rows, cols], in_=y_sb[:, rows, cols])
 
         halves = (slice(0, HALF), slice(HALF, SIZE))
@@ -217,11 +224,12 @@ def tile_nonlocalblocknd_pb_s_kernel(tc, theta_x, phi_x, g_x, out):
         second_product(halves[0], 0)
         quantise_g(1)
         second_product(halves[0], 1)
-        store_y(halves[0], 0, nc.vector.tensor_copy)
-        store_y(halves[0], 1, nc.scalar.copy)
+        store_y(0, 0, nc.vector.tensor_copy)
+        store_y(0, 1, nc.scalar.copy)
         quantise_f(chunks[2])
         quantise_f(chunks[3])
-        second_product(halves[1], 0)
-        second_product(halves[1], 1)
-        store_y(halves[1], 0, nc.vector.tensor_copy)
-        store_y(halves[1], 1, nc.scalar.copy)
+        for cols in chunks[2:]:
+            second_product(cols, 0)
+            second_product(cols, 1)
+        store_y(1, 0, nc.vector.tensor_copy)
+        store_y(1, 1, nc.scalar.copy)

@@ -15,6 +15,7 @@ CHUNK = 128
 N_CHUNKS = SIZE // CHUNK
 HALF = SIZE // 2
 PHI_SPLIT = 88
+THETA_SPLIT = HALF + 192
 WARM_UP_PASSES = 24
 FLOPS = 2 * 2 * SIZE * SIZE * SIZE
 
@@ -191,11 +192,13 @@ def tile_nonlocalblocknd_pb_s_kernel(tc, theta_x, phi_x, g_x, out):
                     stop=True,
                 )
 
-        def store_y(half, b, copy):
+        def store_y(half, b, copy, pieces=1):
             cols = halves[half]
-            rows = slice(2 * b, 2 * b + 2)
-            copy(out=y_sb[:, rows, cols], in_=y_banks[half, b][:])
-            nc.sync.dma_start(out=y[:, rows, cols], in_=y_sb[:, rows, cols])
+            for piece in range(pieces):
+                rows = slice(piece * 2 // pieces, (piece + 1) * 2 // pieces)
+                out_rows = slice(2 * b + rows.start, 2 * b + rows.stop)
+                copy(out=y_sb[:, out_rows, cols], in_=y_banks[half, b][:, rows, :])
+                nc.sync.dma_start(out=y[:, out_rows, cols], in_=y_sb[:, out_rows, cols])
 
         halves = (slice(0, HALF), slice(HALF, SIZE))
         chunks = [slice(k * CHUNK, (k + 1) * CHUNK) for k in range(N_CHUNKS)]
@@ -207,8 +210,8 @@ def tile_nonlocalblocknd_pb_s_kernel(tc, theta_x, phi_x, g_x, out):
         first_product(0)
         first_product(1)
         transpose_g(1)
-        regroup_theta(nc.vector.tensor_copy, chunks[2])
-        regroup_theta(nc.scalar.copy, chunks[3])
+        regroup_theta(nc.vector.tensor_copy, slice(HALF, THETA_SPLIT))
+        regroup_theta(nc.scalar.copy, slice(THETA_SPLIT, SIZE))
         regroup_g(0)
         scale_f(0, True)
         scale_f(1, False)
@@ -219,12 +222,12 @@ def tile_nonlocalblocknd_pb_s_kernel(tc, theta_x, phi_x, g_x, out):
         regroup_g(1)
         quantise_f(chunks[0])
         quantise_f(chunks[1])
-        scale_f(2, False)
-        scale_f(3, False)
         second_product(halves[0], 0)
         quantise_g(1)
         second_product(halves[0], 1)
-        store_y(0, 0, nc.vector.tensor_copy)
+        scale_f(2, False)
+        scale_f(3, True)
+        store_y(0, 0, nc.scalar.copy, pieces=2)
         store_y(0, 1, nc.scalar.copy)
         quantise_f(chunks[2])
         quantise_f(chunks[3])

@@ -72,12 +72,11 @@ def tile_nonlocalblocknd_pb_s_kernel(tc, theta_x, phi_x, g_x, out):
             )
 
         phi_grouped = keep.tile([P, PACK, P, PACK], BF16, align_bytes=64)
-        phi_sorted = phi_raw[:].rearrange("p j (c t) -> p c j t", t=PACK)
-        phi_target = phi_grouped[:].rearrange("p t c j -> p c j t")
+        phi_sorted = phi_raw[:].rearrange("p j (c t) -> p t c j", t=PACK)
         for h in range(2):
             rows = slice(2 * h, 2 * h + 2)
             for copy, columns in ((nc.vector.tensor_copy, slice(0, PHI_SPLIT)), (nc.scalar.copy, slice(PHI_SPLIT, P))):
-                copy(out=phi_target[:, columns, rows, :], in_=phi_sorted[:, columns, rows, :])
+                copy(out=phi_grouped[:, :, columns, rows], in_=phi_sorted[:, :, columns, rows])
         phi_codes = keep.tile([P, PACK, P], U32, align_bytes=64)
         phi_scales = keep.tile([P, PACK, P], U8, align_bytes=64)
 

@@ -72,11 +72,12 @@ def tile_nonlocalblocknd_pb_s_kernel(tc, theta_x, phi_x, g_x, out):
             )
 
         phi_grouped = keep.tile([P, PACK, P, PACK], BF16, align_bytes=64)
-        phi_sorted = phi_raw[:].rearrange("p j (c t) -> p t c j", t=PACK)
+        phi_sorted = phi_raw[:].rearrange("p j (u c e) -> p u e c j", u=2, e=2)
+        phi_planes = phi_grouped[:].rearrange("p (u e) c j -> p u e c j", u=2)
         for h in range(2):
             rows = slice(2 * h, 2 * h + 2)
             for copy, columns in ((nc.vector.tensor_copy, slice(0, PHI_SPLIT)), (nc.scalar.copy, slice(PHI_SPLIT, P))):
-                copy(out=phi_grouped[:, :, columns, rows], in_=phi_sorted[:, :, columns, rows])
+                copy(out=phi_planes[:, :, :, columns, rows], in_=phi_sorted[:, :, :, columns, rows])
         phi_codes = keep.tile([P, PACK, P], U32, align_bytes=64)
         phi_scales = keep.tile([P, PACK, P], U8, align_bytes=64)
 
@@ -117,7 +118,7 @@ def tile_nonlocalblocknd_pb_s_kernel(tc, theta_x, phi_x, g_x, out):
             g_bank = banks.tile([P, 2, 2 * P], F32, tag="bank")
             g_banks[b] = g_bank
             for i in range(2):
-                words = g_rows[:, 2 * b + i, :].bitcast(F32).rearrange("p (c u) -> p u c", u=2)
+                words = g_rows[:, 2 * b + i, :].bitcast(F32).rearrange("p (u c) -> p u c", u=2)
                 for u in range(2):
                     nc.tensor.transpose(g_bank[:, u, i * P : (i + 1) * P], words[:, u, :], identity[:])
 

@@ -175,30 +175,26 @@ def tile_nonlocalblocknd_pb_s_kernel(tc, theta_x, phi_x, g_x, out):
 
         y_banks = {}
 
-        def second_product(cols, b):
+        def second_product(cols, i):
             half = cols.start // HALF
-            if (half, b) not in y_banks:
-                y_bank = banks.tile([P, 2, HALF], F32, tag="bank")
-                y_banks[half, b] = y_bank
+            if (half, i) not in y_banks:
+                y_bank = banks.tile([P, HALF], F32, tag="bank")
+                y_banks[half, i] = y_bank
             first = cols.start - half * HALF
-            for i in range(2):
-                nc.tensor.matmul_mx(
-                    out=y_banks[half, b][:, i, first : first + cols.stop - cols.start],
-                    lhsT=g_codes[:, 2 * b + i, :].bitcast(FP8X4),
-                    lhsT_scale=g_scales[:, 2 * b + i, :],
-                    rhs=f_codes[:, cols].bitcast(FP8X4),
-                    rhs_scale=f_scales[:, cols],
-                    start=True,
-                    stop=True,
-                )
+            nc.tensor.matmul_mx(
+                out=y_banks[half, i][:, first : first + cols.stop - cols.start],
+                lhsT=g_codes[:, i, :].bitcast(FP8X4),
+                lhsT_scale=g_scales[:, i, :],
+                rhs=f_codes[:, cols].bitcast(FP8X4),
+                rhs_scale=f_scales[:, cols],
+                start=True,
+                stop=True,
+            )
 
-        def store_y(half, b, copy, pieces=1):
+        def store_y(half, i, copy):
             cols = halves[half]
-            for piece in range(pieces):
-                rows = slice(piece * 2 // pieces, (piece + 1) * 2 // pieces)
-                out_rows = slice(2 * b + rows.start, 2 * b + rows.stop)
-                copy(out=y_sb[:, out_rows, cols], in_=y_banks[half, b][:, rows, :])
-                nc.sync.dma_start(out=y[:, out_rows, cols], in_=y_sb[:, out_rows, cols])
+            copy(out=y_sb[:, i, cols], in_=y_banks[half, i][:])
+            nc.sync.dma_start(out=y[:, i, cols], in_=y_sb[:, i, cols])
 
         halves = (slice(0, HALF), slice(HALF, SIZE))
         chunks = [slice(k * CHUNK, (k + 1) * CHUNK) for k in range(N_CHUNKS)]
@@ -223,16 +219,18 @@ def tile_nonlocalblocknd_pb_s_kernel(tc, theta_x, phi_x, g_x, out):
         quantise_f(chunks[0])
         quantise_f(chunks[1])
         second_product(halves[0], 0)
-        quantise_g(1)
         second_product(halves[0], 1)
+        quantise_g(1)
+        second_product(halves[0], 2)
+        second_product(halves[0], 3)
         scale_f(2, False)
         scale_f(3, True)
-        store_y(0, 0, nc.scalar.copy, pieces=2)
-        store_y(0, 1, nc.scalar.copy)
+        for i in range(PACK):
+            store_y(0, i, nc.scalar.copy)
         quantise_f(chunks[2])
         quantise_f(chunks[3])
         for cols in chunks[2:]:
-            second_product(cols, 0)
-            second_product(cols, 1)
-        store_y(1, 0, nc.vector.tensor_copy)
-        store_y(1, 1, nc.scalar.copy)
+            for i in range(PACK):
+                second_product(cols, i)
+        for i in range(PACK):
+            store_y(1, i, nc.scalar.copy if i % 2 else nc.vector.tensor_copy)

import concourse.mybir as mybir
from concourse.masks import make_identity

BF16 = mybir.dt.bfloat16
F32 = mybir.dt.float32
U32 = mybir.dt.uint32
U8 = mybir.dt.uint8
FP8X4 = mybir.dt.float8_e4m3fn_x4
COPY = mybir.ActivationFunctionType.Copy

P = 128
PACK = 4
SIZE = 512
CHUNK = 128
N_CHUNKS = SIZE // CHUNK
HALF = SIZE // 2
PHI_SPLIT = 88
THETA_SPLIT = HALF + 192
WARM_UP_PASSES = 24
FLOPS = 2 * 2 * SIZE * SIZE * SIZE


def quantise(nc, grouped, codes, scales):
    nc.vector.quantize_mx(out=codes.bitcast(FP8X4), scales=scales, in_=grouped)


def tile_nonlocalblocknd_pb_s_kernel(tc, theta_x, phi_x, g_x, out):
    nc = tc.nc
    theta = theta_x.flatten_outer_dims().rearrange("(p j) n -> p j n", j=PACK)
    phi = phi_x.flatten_outer_dims().rearrange("(p j) m -> p j m", j=PACK)
    g = g_x.flatten_outer_dims().rearrange("(p i) m -> p i m", i=PACK)
    y = out.flatten_outer_dims().rearrange("(p i) n -> p i n", i=PACK)

    with tc.tile_pool(name="keep", bufs=1) as keep, tc.psum_pool(
        name="banks", bufs=8
    ) as banks, tc.manual_schedule():
        phi_raw = keep.tile([P, PACK, SIZE], BF16)
        for h in range(2):
            rows = slice(2 * h, 2 * h + 2)
            nc.sync.dma_start(out=phi_raw[:, rows, :], in_=phi[:, rows, :])
        g_rows = keep.tile([P, PACK, SIZE], BF16)
        theta_raw = keep.tile([P, PACK, SIZE], BF16)
        for h in range(2):
            cols = slice(h * HALF, (h + 1) * HALF)
            rows = slice(2 * h, 2 * h + 2)
            nc.sync.dma_start(out=theta_raw[:, :, cols], in_=theta[:, :, cols])
            nc.sync.dma_start(out=g_rows[:, rows, :], in_=g[:, rows, :])

        identity = keep.tile([P, P], F32)
        make_identity(nc, identity[:])

        table_in = keep.tile([P, 1], F32)
        table_out = keep.tile([P, 1], F32)
        nc.vector.memset(table_in[:], 0.0)
        nc.scalar.activation(out=table_out[:], in_=table_in[:], func=COPY, scale=1.0)

        idle_grouped = keep.tile([P, PACK * P], BF16, align_bytes=64)
        idle_codes = keep.tile([P, P], U32, align_bytes=64)
        idle_scales = keep.tile([P, P], U8, align_bytes=64)
        nc.vector.memset(idle_grouped[:].bitcast(U32), 0)
        quantise(nc, idle_grouped[:], idle_codes[:], idle_scales[:])
        idle_bank = banks.tile([P, P], F32, tag="bank")
        for w in range(WARM_UP_PASSES):
            nc.tensor.matmul_mx(
                out=idle_bank[:],
                lhsT=idle_codes[:].bitcast(FP8X4),
                lhsT_scale=idle_scales[:],
                rhs=idle_codes[:].bitcast(FP8X4),
                rhs_scale=idle_scales[:],
                start=True,
                stop=True,
            )

        phi_grouped = keep.tile([P, PACK, P, PACK], BF16, align_bytes=64)
        phi_sorted = phi_raw[:].rearrange("p j (u c e) -> p u e c j", u=2, e=2)
        phi_planes = phi_grouped[:].rearrange("p (u e) c j -> p u e c j", u=2)
        for h in range(2):
            rows = slice(2 * h, 2 * h + 2)
            for copy, columns in ((nc.vector.tensor_copy, slice(0, PHI_SPLIT)), (nc.scalar.copy, slice(PHI_SPLIT, P))):
                copy(out=phi_planes[:, :, :, columns, rows], in_=phi_sorted[:, :, :, columns, rows])
        phi_codes = keep.tile([P, PACK, P], U32, align_bytes=64)
        phi_scales = keep.tile([P, PACK, P], U8, align_bytes=64)

        def quantise_phi():
            quantise(
                nc,
                phi_grouped[:].rearrange("p t c j -> p (t c j)"),
                phi_codes[:].rearrange("p t c -> p (t c)"),
                phi_scales[:].rearrange("p t c -> p (t c)"),
            )

        theta_grouped = keep.tile([P, SIZE, PACK], BF16, align_bytes=64)
        theta_codes = keep.tile([P, SIZE], U32, align_bytes=64)
        theta_scales = keep.tile([P, SIZE], U8, align_bytes=64)

        def regroup_theta(copy, cols):
            copy(
                out=theta_grouped[:, cols, :].rearrange("p (c i) j -> p c j i", i=4),
                in_=theta_raw[:, :, cols].rearrange("p j (c i) -> p c j i", i=4),
            )

        def quantise_theta(h):
            cols = slice(h * HALF, (h + 1) * HALF)
            quantise(
                nc,
                theta_grouped[:, cols, :].rearrange("p n j -> p (n j)"),
                theta_codes[:, cols],
                theta_scales[:, cols],
            )

        g_grouped = keep.tile([P, PACK * SIZE], BF16, align_bytes=64)
        g_codes = keep.tile([P, PACK, P], U32, align_bytes=64)
        g_scales = keep.tile([P, PACK, P], U8, align_bytes=64)

        g_banks = {}

        def transpose_g(b):
            g_bank = banks.tile([P, 2, 2 * P], F32, tag="bank")
            g_banks[b] = g_bank
            for i in range(2):
                words = g_rows[:, 2 * b + i, :].bitcast(F32).rearrange("p (u c) -> p u c", u=2)
                for u in range(2):
                    nc.tensor.transpose(g_bank[:, u, i * P : (i + 1) * P], words[:, u, :], identity[:])

        def regroup_g(b):
            nc.scalar.copy(
                out=g_grouped[:, b * 2 * SIZE : (b + 1) * 2 * SIZE]
                .bitcast(F32)
                .rearrange("c (x u) -> c x u", u=2),
                in_=g_banks[b][:].rearrange("c u x -> c x u"),
            )

        def quantise_g(b):
            quantise(
                nc,
                g_grouped[:, b * 2 * SIZE : (b + 1) * 2 * SIZE],
                g_codes[:, 2 * b : 2 * b + 2, :].rearrange("c i p -> c (i p)"),
                g_scales[:, 2 * b : 2 * b + 2, :].rearrange("c i p -> c (i p)"),
            )

        f_grouped = keep.tile([P, SIZE, PACK], BF16, align_bytes=64)
        f_codes = keep.tile([P, SIZE], U32, align_bytes=64)
        f_scales = keep.tile([P, SIZE], U8, align_bytes=64)
        y_sb = keep.tile([P, PACK, SIZE], F32)

        f_banks = {}

        def first_product(k):
            cols = slice(k * CHUNK, (k + 1) * CHUNK)
            f_bank = banks.tile([P, PACK, CHUNK], F32, tag="bank")
            f_banks[k] = f_bank
            for t in range(PACK):
                nc.tensor.matmul_mx(
                    out=f_bank[:, t, :],
                    lhsT=phi_codes[:, t, :].bitcast(FP8X4),
                    lhsT_scale=phi_scales[:, t, :],
                    rhs=theta_codes[:, cols].bitcast(FP8X4),
                    rhs_scale=theta_scales[:, cols],
                    start=True,
                    stop=True,
                )

        def scale_f(k, on_vector):
            cols = slice(k * CHUNK, (k + 1) * CHUNK)
            source = f_banks[k][:].rearrange("c t n -> c n t")
            if on_vector:
                nc.vector.tensor_scalar_mul(out=f_grouped[:, cols, :], in0=source, scalar1=1.0 / SIZE)
            else:
                nc.scalar.activation(out=f_grouped[:, cols, :], in_=source, func=COPY, scale=1.0 / SIZE)

        def quantise_f(cols):
            quantise(
                nc, f_grouped[:, cols, :].rearrange("c n t -> c (n t)"), f_codes[:, cols], f_scales[:, cols]
            )

        y_banks = {}

        def second_product(cols, i):
            half = cols.start // HALF
            if (half, i) not in y_banks:
                y_bank = banks.tile([P, HALF], F32, tag="bank")
                y_banks[half, i] = y_bank
            first = cols.start - half * HALF
            nc.tensor.matmul_mx(
                out=y_banks[half, i][:, first : first + cols.stop - cols.start],
                lhsT=g_codes[:, i, :].bitcast(FP8X4),
                lhsT_scale=g_scales[:, i, :],
                rhs=f_codes[:, cols].bitcast(FP8X4),
                rhs_scale=f_scales[:, cols],
                start=True,
                stop=True,
            )

        def store_y(half, i, copy):
            cols = halves[half]
            copy(out=y_sb[:, i, cols], in_=y_banks[half, i][:])
            nc.sync.dma_start(out=y[:, i, cols], in_=y_sb[:, i, cols])

        halves = (slice(0, HALF), slice(HALF, SIZE))
        chunks = [slice(k * CHUNK, (k + 1) * CHUNK) for k in range(N_CHUNKS)]
        regroup_theta(nc.vector.tensor_copy, chunks[0])
        regroup_theta(nc.scalar.copy, chunks[1])
        quantise_phi()
        quantise_theta(0)
        transpose_g(0)
        first_product(0)
        first_product(1)
        transpose_g(1)
        regroup_theta(nc.vector.tensor_copy, slice(HALF, THETA_SPLIT))
        regroup_theta(nc.scalar.copy, slice(THETA_SPLIT, SIZE))
        regroup_g(0)
        scale_f(0, True)
        scale_f(1, False)
        quantise_theta(1)
        quantise_g(0)
        first_product(2)
        first_product(3)
        regroup_g(1)
        quantise_f(chunks[0])
        quantise_f(chunks[1])
        second_product(halves[0], 0)
        second_product(halves[0], 1)
        quantise_g(1)
        second_product(halves[0], 2)
        second_product(halves[0], 3)
        scale_f(2, False)
        scale_f(3, True)
        for i in range(PACK):
            store_y(0, i, nc.scalar.copy)
        quantise_f(chunks[2])
        quantise_f(chunks[3])
        for cols in chunks[2:]:
            for i in range(PACK):
                second_product(cols, i)
        for i in range(PACK):
            store_y(1, i, nc.scalar.copy if i % 2 else nc.vector.tensor_copy)
